import numpy as np
import ml_dtypes


def mxq(x, axis, fmt="e4m3"):
    dtype, down = {"e4m3": (ml_dtypes.float8_e4m3fn, 7), "e5m2": (ml_dtypes.float8_e5m2, 14)}[fmt]
    v = np.moveaxis(np.asarray(x, np.float32).astype(ml_dtypes.bfloat16).astype(np.float64), axis, -1)
    blocks = v.reshape(v.shape[:-1] + (-1, 32))
    amax = np.abs(blocks).max(-1, keepdims=True)
    byte = np.maximum(np.where(amax > 0, np.frexp(amax)[1] - 1 + 127, 0) - down, 1)
    scale = np.exp2(byte - 127.0)
    codes = (blocks / scale).astype(np.float32).astype(dtype).astype(np.float64)
    return np.moveaxis((codes * scale).reshape(v.shape), -1, axis)


WIDE = False


def mx_kscale(k):
    if not WIDE:
        return np.ones(k)
    levels = np.array([10, -10, 5, -5, 0])
    a = np.random.permutation(np.resize(levels, k // 512 * 4)).reshape(k // 512, 4)
    idx = np.arange(k)
    return np.exp2(a[idx // 512, idx % 128 // 32])


BF16 = ml_dtypes.bfloat16


def bf(x):
    return np.asarray(x, np.float32).astype(BF16)


def f64(x):
    return np.asarray(x).astype(np.float64)


B, C, HD, H, W = 2, 512, 128, 32, 32
N = H * W
C2 = 2 * C
C3 = 3 * C


def sigmoid(v):
    return 1.0 / (1.0 + np.exp(-v))


def setup_inputs():
    s = mx_kscale(C3)
    return {
        "z": bf(np.random.standard_normal((B, C2, H, W)) * s[None, :C2, None, None]),
        "h": bf(np.random.standard_normal((B, C, H, W)) * s[None, C2:, None, None]),
        "m": bf(np.random.standard_normal((B, C, H, W))),
        "Wm": bf(np.random.standard_normal((C3, C3)) * 1.5 / np.sqrt(C3) / s[None, :]),
        "bm": bf(np.random.standard_normal(C3) * 0.3),
    }


def reference(z, h, m, Wm, bm):
    x = np.concatenate([f64(z), f64(h)], axis=1).reshape(B, C3, N)
    combined = ((mxq(f64(Wm), 1, "e4m3") @ mxq(x, 1, "e4m3")) + f64(bm)[None, :, None]).reshape(B, C3, H, W)
    mo, mg, mi = combined[:, :C], combined[:, C:C2], combined[:, C2:]
    mi = sigmoid(mi)
    new_m = (1.0 - mi) * f64(m) + mi * np.tanh(mg)
    new_h = sigmoid(mo) * new_m
    return new_h, new_m

@@ -1,0 +1,237 @@
+from contextlib import ExitStack
+
+import concourse.mybir as mybir
+from concourse.masks import make_identity
+
+F32 = mybir.dt.float32
+BF16 = mybir.dt.bfloat16
+U32 = mybir.dt.uint32
+U8 = mybir.dt.uint8
+FP8X4 = mybir.dt.float8_e4m3fn_x4
+ACT = mybir.ActivationFunctionType
+
+P = 128
+PACK = 4
+K_PASS = P * PACK
+BATCH = 2
+C = 512
+C3 = 3 * C
+PIXELS = 1024
+PASSES = C3 // K_PASS
+GATES = 3
+OUT_GATE, CANDIDATE, IN_GATE = 0, 1, 2
+C_TILES = C // P
+N_TILE = 512
+N_TILES = BATCH * PIXELS // N_TILE
+HALVES = PIXELS // N_TILE
+W_CHUNKS = GATES * C_TILES * PASSES
+CHUNKS_PER_BANK = 2
+RUN = 4
+
+FLOPS = 2 * C3 * C3 * BATCH * PIXELS
+
+
+def tile_self_attention_memory_module_pb_kernel(tc, z, h, m, Wm, bm, out_0, out_1):
+    nc = tc.nc
+
+    z_rows = z.rearrange("b c i j -> b c (i j)")
+    h_rows = h.rearrange("b c i j -> b c (i j)")
+    m_tiles = m.rearrange("b (t p) i j -> b p t (i j)", p=P)
+    new_h_rows = out_0.rearrange("b c i j -> b c (i j)")
+    new_m_rows = out_1.rearrange("b c i j -> b c (i j)")
+    w_groups = Wm.rearrange("(a t p) k -> t p a k", a=GATES, t=C_TILES, p=P)
+
+    def pass_rows(b, g):
+        if g < 2:
+            return z_rows[b, g * K_PASS : (g + 1) * K_PASS, :]
+        return h_rows[b]
+
+    def pixels_of(n):
+        b, half = divmod(n, HALVES)
+        return b, slice(half * N_TILE, (half + 1) * N_TILE)
+
+    with ExitStack() as ctx:
+        consts = ctx.enter_context(tc.tile_pool(name="consts", bufs=1))
+        resident = ctx.enter_context(tc.tile_pool(name="resident", bufs=1))
+        stage = ctx.enter_context(tc.tile_pool(name="stage", bufs=3))
+        gates = ctx.enter_context(tc.tile_pool(name="gates", bufs=4))
+        psum_w = ctx.enter_context(tc.psum_pool(name="psum_w", bufs=2))
+        psum_acc = ctx.enter_context(tc.psum_pool(name="psum_acc", bufs=2))
+
+        w_raw = resident.tile([P, GATES * C_TILES, C3], BF16)
+        x_raw = [
+            resident.tile([P, PASSES, PACK, N_TILE], BF16, name="x_raw%d" % n)
+            for n in range(N_TILES)
+        ]
+        m_sb = [
+            resident.tile([P, C_TILES, N_TILE], BF16, name="m_sb%d" % n) for n in range(N_TILES)
+        ]
+        w_codes = resident.tile([P, W_CHUNKS * P], U32, align_bytes=64)
+        w_scales = resident.tile([P, W_CHUNKS * P], U8, align_bytes=64)
+        x_codes = [
+            resident.tile([P, PASSES * N_TILE], U32, name="x_codes%d" % n, align_bytes=64)
+            for n in range(N_TILES)
+        ]
+        x_scales = [
+            resident.tile([P, PASSES * N_TILE], U8, name="x_scales%d" % n, align_bytes=64)
+            for n in range(N_TILES)
+        ]
+
+        def load_w(t):
+            nc.sync.dma_start(out=w_raw[:, GATES * t : GATES * (t + 1), :], in_=w_groups[t])
+
+        def load_x(n):
+            b, cols = pixels_of(n)
+            for g in range(PASSES):
+                for u in range(2):
+                    rows = pass_rows(b, g)[u * 2 * P : (u + 1) * 2 * P, cols]
+                    nc.sync.dma_start(
+                        out=x_raw[n][:, g, 2 * u : 2 * u + 2, :],
+                        in_=rows.rearrange("(p e) w -> p e w", e=2),
+                    )
+
+        def load_m(n):
+            b, cols = pixels_of(n)
+            nc.sync.dma_start(out=m_sb[n][:], in_=m_tiles[b][:, :, cols])
+
+        bias_in = consts.tile([GATES * C_TILES, P], BF16)
+        nc.scalar.dma_start(out=bias_in[:], in_=bm.rearrange("(r c) -> r c", c=P))
+        load_w(0)
+        load_x(0)
+        load_w(1)
+        load_m(0)
+        load_w(2)
+        load_w(3)
+        for n in range(1, N_TILES):
+            load_x(n)
+            load_m(n)
+
+        warm = consts.tile([P, 1], F32)
+        nc.vector.memset(warm[:], 0.0)
+        warm_out = consts.tile([P, 1], F32)
+        nc.scalar.activation(out=warm_out[:], in_=warm[:], func=ACT.Sigmoid)
+
+        ident = consts.tile([P, P], F32)
+        make_identity(nc, ident[:])
+
+        bias_rows = consts.tile([P, P], F32)
+        nc.vector.memset(bias_rows[:], 0.0)
+        nc.vector.tensor_copy(out=bias_rows[0 : GATES * C_TILES, :], in_=bias_in[:])
+        bias_turned = psum_w.tile([P, CHUNKS_PER_BANK, 2, P], F32, tag="w_turned")
+        nc.tensor.transpose(bias_turned[:, 0, 0, :], bias_rows[:], ident[:])
+        bias = consts.tile([P, GATES * C_TILES], F32)
+        nc.vector.tensor_copy(out=bias[:], in_=bias_turned[:, 0, 0, 0 : GATES * C_TILES])
+
+        def chunk_of(t, a, g):
+            return (t * GATES + a) * PASSES + g
+
+        def turn_w_bank(j):
+            w_turned = psum_w.tile([P, CHUNKS_PER_BANK, 2, P], F32, tag="w_turned")
+            for s in range(CHUNKS_PER_BANK):
+                row_tile, g = divmod(j * CHUNKS_PER_BANK + s, PASSES)
+                words = w_raw[:, row_tile, :].bitcast(F32)
+                for u in range(2):
+                    first = g * 2 * P + u * P
+                    nc.tensor.transpose(w_turned[:, s, u, :], words[:, first : first + P], ident[:])
+            w_grouped = stage.tile([P, CHUNKS_PER_BANK * P * PACK], BF16, align_bytes=64)
+            nc.scalar.copy(
+                out=w_grouped[:].bitcast(F32).rearrange("p (s o u) -> p s o u", s=CHUNKS_PER_BANK, u=2),
+                in_=w_turned[:].rearrange("p s u o -> p s o u"),
+            )
+            cols = slice(j * CHUNKS_PER_BANK * P, (j + 1) * CHUNKS_PER_BANK * P)
+            nc.vector.quantize_mx(
+                out=w_codes[:, cols].bitcast(FP8X4), scales=w_scales[:, cols], in_=w_grouped[:]
+            )
+
+        def banks_for(t):
+            chunks = (t + 1) * GATES * PASSES
+            return (chunks + CHUNKS_PER_BANK - 1) // CHUNKS_PER_BANK
+
+        def prepare_x(n, g):
+            copy = nc.vector.tensor_copy if n < HALVES else nc.scalar.copy
+            x_grouped = stage.tile([P, N_TILE, PACK], BF16, align_bytes=64)
+            copy(
+                out=x_grouped[:].rearrange("p (c i) t -> p c t i", i=RUN),
+                in_=x_raw[n][:, g, :, :].rearrange("p t (c i) -> p c t i", i=RUN),
+            )
+            cols = slice(g * N_TILE, (g + 1) * N_TILE)
+            nc.vector.quantize_mx(
+                out=x_codes[n][:, cols].bitcast(FP8X4),
+                scales=x_scales[n][:, cols],
+                in_=x_grouped[:].rearrange("p w t -> p (w t)"),
+            )
+
+        def multiply(n, t, a, name):
+            acc = psum_acc.tile([P, N_TILE], F32, name=name)
+            for g in range(PASSES):
+                w_cols = slice(chunk_of(t, a, g) * P, (chunk_of(t, a, g) + 1) * P)
+                x_cols = slice(g * N_TILE, (g + 1) * N_TILE)
+                nc.tensor.matmul_mx(
+                    out=acc[:],
+                    lhsT=w_codes[:, w_cols].bitcast(FP8X4),
+                    lhsT_scale=w_scales[:, w_cols],
+                    rhs=x_codes[n][:, x_cols].bitcast(FP8X4),
+                    rhs_scale=x_scales[n][:, x_cols],
+                    start=(g == 0),
+                    stop=(g == PASSES - 1),
+                )
+            return acc
+
+        def squash(acc, func, t, a, name):
+            r = a * C_TILES + t
+            result = gates.tile([P, N_TILE], F32, name=name)
+            nc.scalar.activation(out=result[:], in_=acc[:], func=func, bias=bias[:, r : r + 1], scale=1.0)
+            return result
+
+        def gates_of(n, t):
+            acc_g = multiply(n, t, CANDIDATE, "acc_g")
+            acc_i = multiply(n, t, IN_GATE, "acc_i")
+            acc_o = multiply(n, t, OUT_GATE, "acc_o")
+            return {
+                "n": n,
+                "t": t,
+                "cand": squash(acc_g, ACT.Tanh, t, CANDIDATE, "cand"),
+                "gate_i": squash(acc_i, ACT.Sigmoid, t, IN_GATE, "gate_i"),
+                "gate_o": squash(acc_o, ACT.Sigmoid, t, OUT_GATE, "gate_o"),
+            }
+
+        def difference(unit):
+            nc.vector.tensor_sub(out=unit["cand"][:], in0=unit["cand"][:], in1=m_sb[unit["n"]][:, unit["t"], :])
+
+        def gated_step(unit):
+            nc.vector.tensor_mul(out=unit["cand"][:], in0=unit["gate_i"][:], in1=unit["cand"][:])
+
+        def store(rows, unit, result):
+            b, cols = pixels_of(unit["n"])
+            nc.sync.dma_start(out=rows[b, unit["t"] * P : (unit["t"] + 1) * P, cols], in_=result[:])
+
+        def new_memory(unit):
+            new_m = gates.tile([P, N_TILE], F32, name="new_m")
+            nc.vector.tensor_add(out=new_m[:], in0=unit["cand"][:], in1=m_sb[unit["n"]][:, unit["t"], :])
+            store(new_m_rows, unit, new_m)
+            return new_m
+
+        def new_hidden(unit, new_m):
+            nc.vector.tensor_mul(out=unit["gate_o"][:], in0=unit["gate_o"][:], in1=new_m[:])
+            store(new_h_rows, unit, unit["gate_o"])
+
+        for g in range(PASSES):
+            prepare_x(0, g)
+
+        earlier = None
+        for n in range(N_TILES):
+            for t in range(C_TILES):
+                if n == 0:
+                    for j in range(banks_for(t - 1), banks_for(t)):
+                        turn_w_bank(j)
+                unit = gates_of(n, t)
+                if n + 1 < N_TILES and t < PASSES:
+                    prepare_x(n + 1, t)
+                difference(unit)
+                if earlier is not None:
+                    new_m = new_memory(earlier)
+                gated_step(unit)
+                if earlier is not None:
+                    new_hidden(earlier, new_m)
+                earlier = unit
+        new_hidden(earlier, new_memory(earlier))

@@ -18,14 +18,17 @@ C = 512
 C3 = 3 * C
 PIXELS = 1024
 PASSES = C3 // K_PASS
+Z_PASSES = 2
 GATES = 3
 OUT_GATE, CANDIDATE, IN_GATE = 0, 1, 2
 C_TILES = C // P
 N_TILE = 512
 N_TILES = BATCH * PIXELS // N_TILE
 HALVES = PIXELS // N_TILE
+PSUM_BANKS = 8
 W_CHUNKS = GATES * C_TILES * PASSES
 CHUNKS_PER_BANK = 2
+W_BANKS = W_CHUNKS // CHUNKS_PER_BANK
 RUN = 4
 
 FLOPS = 2 * C3 * C3 * BATCH * PIXELS
@@ -36,13 +39,13 @@ def tile_self_attention_memory_module_pb_kernel(tc, z, h, m, Wm, bm, out_0, out_
 
     z_rows = z.rearrange("b c i j -> b c (i j)")
     h_rows = h.rearrange("b c i j -> b c (i j)")
-    m_tiles = m.rearrange("b (t p) i j -> b p t (i j)", p=P)
-    new_h_rows = out_0.rearrange("b c i j -> b c (i j)")
-    new_m_rows = out_1.rearrange("b c i j -> b c (i j)")
-    w_groups = Wm.rearrange("(a t p) k -> t p a k", a=GATES, t=C_TILES, p=P)
+    m_tiles = m.rearrange("b (q r) i j -> b q r (i j)", r=C_TILES)
+    new_h_tiles = out_0.rearrange("b (q r) i j -> b q r (i j)", r=C_TILES)
+    new_m_tiles = out_1.rearrange("b (q r) i j -> b q r (i j)", r=C_TILES)
+    w_tiles = Wm.rearrange("(a q r) k -> a q r k", a=GATES, r=C_TILES)
 
     def pass_rows(b, g):
-        if g < 2:
+        if g < Z_PASSES:
             return z_rows[b, g * K_PASS : (g + 1) * K_PASS, :]
         return h_rows[b]
 
@@ -54,11 +57,10 @@ def tile_self_attention_memory_module_pb_kernel(tc, z, h, m, Wm, bm, out_0, out_
         consts = ctx.enter_context(tc.tile_pool(name="consts", bufs=1))
         resident = ctx.enter_context(tc.tile_pool(name="resident", bufs=1))
         stage = ctx.enter_context(tc.tile_pool(name="stage", bufs=3))
-        gates = ctx.enter_context(tc.tile_pool(name="gates", bufs=4))
-        psum_w = ctx.enter_context(tc.psum_pool(name="psum_w", bufs=2))
-        psum_acc = ctx.enter_context(tc.psum_pool(name="psum_acc", bufs=2))
+        gates = ctx.enter_context(tc.tile_pool(name="gates", bufs=6))
+        psum = ctx.enter_context(tc.psum_pool(name="psum", bufs=PSUM_BANKS))
 
-        w_raw = resident.tile([P, GATES * C_TILES, C3], BF16)
+        w_raw = resident.tile([P, GATES, C_TILES, C3], BF16)
         x_raw = [
             resident.tile([P, PASSES, PACK, N_TILE], BF16, name="x_raw%d" % n)
             for n in range(N_TILES)
@@ -77,8 +79,9 @@ def tile_self_attention_memory_module_pb_kernel(tc, z, h, m, Wm, bm, out_0, out_
             for n in range(N_TILES)
         ]
 
-        def load_w(t):
-            nc.sync.dma_start(out=w_raw[:, GATES * t : GATES * (t + 1), :], in_=w_groups[t])
+        def load_w(a, first_tile):
+            tiles = slice(first_tile, first_tile + 2)
+            nc.sync.dma_start(out=w_raw[:, a, tiles, :], in_=w_tiles[a][:, tiles, :])
 
         def load_x(n):
             b, cols = pixels_of(n)
@@ -94,15 +97,12 @@ def tile_self_attention_memory_module_pb_kernel(tc, z, h, m, Wm, bm, out_0, out_
             b, cols = pixels_of(n)
             nc.sync.dma_start(out=m_sb[n][:], in_=m_tiles[b][:, :, cols])
 
-        bias_in = consts.tile([GATES * C_TILES, P], BF16)
-        nc.scalar.dma_start(out=bias_in[:], in_=bm.rearrange("(r c) -> r c", c=P))
-        load_w(0)
-        load_x(0)
-        load_w(1)
-        load_m(0)
-        load_w(2)
-        load_w(3)
-        for n in range(1, N_TILES):
+        bias_in = consts.tile([P, GATES, C_TILES], BF16)
+        nc.scalar.dma_start(out=bias_in[:], in_=bm.rearrange("(a q r) -> q a r", a=GATES, r=C_TILES))
+        for a in range(GATES):
+            for first_tile in range(0, C_TILES, 2):
+                load_w(a, first_tile)
+        for n in range(N_TILES):
             load_x(n)
             load_m(n)
 
@@ -114,22 +114,18 @@ def tile_self_attention_memory_module_pb_kernel(tc, z, h, m, Wm, bm, out_0, out_
         ident = consts.tile([P, P], F32)
         make_identity(nc, ident[:])
 
-        bias_rows = consts.tile([P, P], F32)
-        nc.vector.memset(bias_rows[:], 0.0)
-        nc.vector.tensor_copy(out=bias_rows[0 : GATES * C_TILES, :], in_=bias_in[:])
-        bias_turned = psum_w.tile([P, CHUNKS_PER_BANK, 2, P], F32, tag="w_turned")
-        nc.tensor.transpose(bias_turned[:, 0, 0, :], bias_rows[:], ident[:])
-        bias = consts.tile([P, GATES * C_TILES], F32)
-        nc.vector.tensor_copy(out=bias[:], in_=bias_turned[:, 0, 0, 0 : GATES * C_TILES])
+        bias = consts.tile([P, GATES, C_TILES], F32)
+        nc.vector.tensor_copy(out=bias[:], in_=bias_in[:])
 
-        def chunk_of(t, a, g):
-            return (t * GATES + a) * PASSES + g
+        def chunk_of(a, r, g):
+            return (a * C_TILES + r) * PASSES + g
 
         def turn_w_bank(j):
-            w_turned = psum_w.tile([P, CHUNKS_PER_BANK, 2, P], F32, tag="w_turned")
+            w_turned = psum.tile([P, CHUNKS_PER_BANK, 2, P], F32, tag="bank")
             for s in range(CHUNKS_PER_BANK):
                 row_tile, g = divmod(j * CHUNKS_PER_BANK + s, PASSES)
-                words = w_raw[:, row_tile, :].bitcast(F32)
+                a, r = divmod(row_tile, C_TILES)
+                words = w_raw[:, a, r, :].bitcast(F32)
                 for u in range(2):
                     first = g * 2 * P + u * P
                     nc.tensor.transpose(w_turned[:, s, u, :], words[:, first : first + P], ident[:])
@@ -138,22 +134,24 @@ def tile_self_attention_memory_module_pb_kernel(tc, z, h, m, Wm, bm, out_0, out_
                 out=w_grouped[:].bitcast(F32).rearrange("p (s o u) -> p s o u", s=CHUNKS_PER_BANK, u=2),
                 in_=w_turned[:].rearrange("p s u o -> p s o u"),
             )
+            return w_grouped
+
+        def quantise_w(j, w_grouped):
             cols = slice(j * CHUNKS_PER_BANK * P, (j + 1) * CHUNKS_PER_BANK * P)
             nc.vector.quantize_mx(
                 out=w_codes[:, cols].bitcast(FP8X4), scales=w_scales[:, cols], in_=w_grouped[:]
             )
 
-        def banks_for(t):
-            chunks = (t + 1) * GATES * PASSES
-            return (chunks + CHUNKS_PER_BANK - 1) // CHUNKS_PER_BANK
-
-        def prepare_x(n, g):
+        def regroup_x(n, g):
             copy = nc.vector.tensor_copy if n < HALVES else nc.scalar.copy
             x_grouped = stage.tile([P, N_TILE, PACK], BF16, align_bytes=64)
             copy(
                 out=x_grouped[:].rearrange("p (c i) t -> p c t i", i=RUN),
                 in_=x_raw[n][:, g, :, :].rearrange("p t (c i) -> p c t i", i=RUN),
             )
+            return x_grouped
+
+        def quantise_x(n, g, x_grouped):
             cols = slice(g * N_TILE, (g + 1) * N_TILE)
             nc.vector.quantize_mx(
                 out=x_codes[n][:, cols].bitcast(FP8X4),
@@ -161,10 +159,10 @@ def tile_self_attention_memory_module_pb_kernel(tc, z, h, m, Wm, bm, out_0, out_
                 in_=x_grouped[:].rearrange("p w t -> p (w t)"),
             )
 
-        def multiply(n, t, a, name):
-            acc = psum_acc.tile([P, N_TILE], F32, name=name)
+        def multiply(n, r, a):
+            acc = psum.tile([P, N_TILE], F32, tag="bank")
             for g in range(PASSES):
-                w_cols = slice(chunk_of(t, a, g) * P, (chunk_of(t, a, g) + 1) * P)
+                w_cols = slice(chunk_of(a, r, g) * P, (chunk_of(a, r, g) + 1) * P)
                 x_cols = slice(g * N_TILE, (g + 1) * N_TILE)
                 nc.tensor.matmul_mx(
                     out=acc[:],
@@ -177,56 +175,66 @@ def tile_self_attention_memory_module_pb_kernel(tc, z, h, m, Wm, bm, out_0, out_
                 )
             return acc
 
-        def squash(acc, func, t, a, name):
-            r = a * C_TILES + t
+        def squash(acc, func, r, a, name):
             result = gates.tile([P, N_TILE], F32, name=name)
-            nc.scalar.activation(out=result[:], in_=acc[:], func=func, bias=bias[:, r : r + 1], scale=1.0)
+            nc.scalar.activation(out=result[:], in_=acc[:], func=func, bias=bias[:, a, r : r + 1], scale=1.0)
             return result
 
-        def gates_of(n, t):
-            acc_g = multiply(n, t, CANDIDATE, "acc_g")
-            acc_i = multiply(n, t, IN_GATE, "acc_i")
-            acc_o = multiply(n, t, OUT_GATE, "acc_o")
+        def gates_of(n, r):
+            acc_g = multiply(n, r, CANDIDATE)
+            acc_i = multiply(n, r, IN_GATE)
+            acc_o = multiply(n, r, OUT_GATE)
             return {
                 "n": n,
-                "t": t,
-                "cand": squash(acc_g, ACT.Tanh, t, CANDIDATE, "cand"),
-                "gate_i": squash(acc_i, ACT.Sigmoid, t, IN_GATE, "gate_i"),
-                "gate_o": squash(acc_o, ACT.Sigmoid, t, OUT_GATE, "gate_o"),
+                "r": r,
+                "cand": squash(acc_g, ACT.Tanh, r, CANDIDATE, "cand"),
+                "gate_i": squash(acc_i, ACT.Sigmoid, r, IN_GATE, "gate_i"),
+                "gate_o": squash(acc_o, ACT.Sigmoid, r, OUT_GATE, "gate_o"),
             }
 
         def difference(unit):
-            nc.vector.tensor_sub(out=unit["cand"][:], in0=unit["cand"][:], in1=m_sb[unit["n"]][:, unit["t"], :])
+            nc.vector.tensor_sub(out=unit["cand"][:], in0=unit["cand"][:], in1=m_sb[unit["n"]][:, unit["r"], :])
 
         def gated_step(unit):
             nc.vector.tensor_mul(out=unit["cand"][:], in0=unit["gate_i"][:], in1=unit["cand"][:])
 
-        def store(rows, unit, result):
+        def store(tiles, unit, result):
             b, cols = pixels_of(unit["n"])
-            nc.sync.dma_start(out=rows[b, unit["t"] * P : (unit["t"] + 1) * P, cols], in_=result[:])
+            nc.sync.dma_start(out=tiles[b][:, unit["r"], cols], in_=result[:])
 
         def new_memory(unit):
             new_m = gates.tile([P, N_TILE], F32, name="new_m")
-            nc.vector.tensor_add(out=new_m[:], in0=unit["cand"][:], in1=m_sb[unit["n"]][:, unit["t"], :])
-            store(new_m_rows, unit, new_m)
+            nc.vector.tensor_add(out=new_m[:], in0=unit["cand"][:], in1=m_sb[unit["n"]][:, unit["r"], :])
+            store(new_m_tiles, unit, new_m)
             return new_m
 
         def new_hidden(unit, new_m):
             nc.vector.tensor_mul(out=unit["gate_o"][:], in0=unit["gate_o"][:], in1=new_m[:])
-            store(new_h_rows, unit, unit["gate_o"])
+            store(new_h_tiles, unit, unit["gate_o"])
 
+        copied = None
+        for j in range(W_BANKS):
+            w_grouped = turn_w_bank(j)
+            if copied is not None:
+                quantise_w(*copied)
+            copied = (j, w_grouped)
+        quantise_w(*copied)
+        copied = None
         for g in range(PASSES):
-            prepare_x(0, g)
+            x_grouped = regroup_x(0, g)
+            if copied is not None:
+                quantise_x(*copied)
+            copied = (0, g, x_grouped)
 
         earlier = None
         for n in range(N_TILES):
-            for t in range(C_TILES):
-                if n == 0:
-                    for j in range(banks_for(t - 1), banks_for(t)):
-                        turn_w_bank(j)
-                unit = gates_of(n, t)
-                if n + 1 < N_TILES and t < PASSES:
-                    prepare_x(n + 1, t)
+            for r in range(C_TILES):
+                if copied is not None:
+                    quantise_x(*copied)
+                    copied = None
+                unit = gates_of(n, r)
+                if n + 1 < N_TILES and r < PASSES:
+                    copied = (n + 1, r, regroup_x(n + 1, r))
                 difference(unit)
                 if earlier is not None:
                     new_m = new_memory(earlier)

@@ -143,7 +143,7 @@ def tile_self_attention_memory_module_pb_kernel(tc, z, h, m, Wm, bm, out_0, out_
             )
 
         def regroup_x(n, g):
-            copy = nc.vector.tensor_copy if n < HALVES else nc.scalar.copy
+            copy = nc.scalar.copy if g < Z_PASSES else nc.vector.tensor_copy
             x_grouped = stage.tile([P, N_TILE, PACK], BF16, align_bytes=64)
             copy(
                 out=x_grouped[:].rearrange("p (c i) t -> p c t i", i=RUN),

@@ -29,6 +29,8 @@ PSUM_BANKS = 8
 W_CHUNKS = GATES * C_TILES * PASSES
 CHUNKS_PER_BANK = 2
 W_BANKS = W_CHUNKS // CHUNKS_PER_BANK
+HEAD_STEPS = 3
+assert HEAD_STEPS == PASSES and HEAD_STEPS == GATES
 RUN = 4
 
 FLOPS = 2 * C3 * C3 * BATCH * PIXELS
@@ -62,12 +64,9 @@ def tile_self_attention_memory_module_pb_kernel(tc, z, h, m, Wm, bm, out_0, out_
 
         w_raw = resident.tile([P, GATES, C_TILES, C3], BF16)
         x_raw = [
-            resident.tile([P, PASSES, PACK, N_TILE], BF16, name="x_raw%d" % n)
-            for n in range(N_TILES)
+            resident.tile([P, PASSES, PACK, PIXELS], BF16, name="x_raw%d" % b) for b in range(BATCH)
         ]
-        m_sb = [
-            resident.tile([P, C_TILES, N_TILE], BF16, name="m_sb%d" % n) for n in range(N_TILES)
-        ]
+        m_sb = [resident.tile([P, C_TILES, PIXELS], BF16, name="m_sb%d" % b) for b in range(BATCH)]
         w_codes = resident.tile([P, W_CHUNKS * P], U32, align_bytes=64)
         w_scales = resident.tile([P, W_CHUNKS * P], U8, align_bytes=64)
         x_codes = [
@@ -79,32 +78,29 @@ def tile_self_attention_memory_module_pb_kernel(tc, z, h, m, Wm, bm, out_0, out_
             for n in range(N_TILES)
         ]
 
-        def load_w(a, first_tile):
-            tiles = slice(first_tile, first_tile + 2)
-            nc.sync.dma_start(out=w_raw[:, a, tiles, :], in_=w_tiles[a][:, tiles, :])
+        def load_w(a):
+            for first_tile in range(0, C_TILES, 2):
+                tiles = slice(first_tile, first_tile + 2)
+                nc.sync.dma_start(out=w_raw[:, a, tiles, :], in_=w_tiles[a][:, tiles, :])
 
-        def load_x(n):
-            b, cols = pixels_of(n)
-            for g in range(PASSES):
-                for u in range(2):
-                    rows = pass_rows(b, g)[u * 2 * P : (u + 1) * 2 * P, cols]
-                    nc.sync.dma_start(
-                        out=x_raw[n][:, g, 2 * u : 2 * u + 2, :],
-                        in_=rows.rearrange("(p e) w -> p e w", e=2),
-                    )
+        def load_x(b, g):
+            nc.sync.dma_start(
+                out=x_raw[b][:, g, :, :].rearrange("p (u e) w -> p u (e w)", u=2),
+                in_=pass_rows(b, g).rearrange("(u p e) w -> p u (e w)", u=2, e=2),
+            )
 
-        def load_m(n):
-            b, cols = pixels_of(n)
-            nc.sync.dma_start(out=m_sb[n][:], in_=m_tiles[b][:, :, cols])
+        def load_m(b):
+            nc.sync.dma_start(out=m_sb[b][:], in_=m_tiles[b])
 
         bias_in = consts.tile([P, GATES, C_TILES], BF16)
         nc.scalar.dma_start(out=bias_in[:], in_=bm.rearrange("(a q r) -> q a r", a=GATES, r=C_TILES))
-        for a in range(GATES):
-            for first_tile in range(0, C_TILES, 2):
-                load_w(a, first_tile)
-        for n in range(N_TILES):
-            load_x(n)
-            load_m(n)
+        for step in range(HEAD_STEPS):
+            load_x(0, step)
+            load_w(step)
+        load_m(0)
+        for g in range(PASSES):
+            load_x(1, g)
+        load_m(1)
 
         warm = consts.tile([P, 1], F32)
         nc.vector.memset(warm[:], 0.0)
@@ -143,11 +139,12 @@ def tile_self_attention_memory_module_pb_kernel(tc, z, h, m, Wm, bm, out_0, out_
             )
 
         def regroup_x(n, g):
-            copy = nc.scalar.copy if g < Z_PASSES else nc.vector.tensor_copy
+            copy = nc.vector.tensor_copy if n < HALVES else nc.scalar.copy
+            b, cols = pixels_of(n)
             x_grouped = stage.tile([P, N_TILE, PACK], BF16, align_bytes=64)
             copy(
                 out=x_grouped[:].rearrange("p (c i) t -> p c t i", i=RUN),
-                in_=x_raw[n][:, g, :, :].rearrange("p t (c i) -> p c t i", i=RUN),
+                in_=x_raw[b][:, g, :, cols].rearrange("p t (c i) -> p c t i", i=RUN),
             )
             return x_grouped
 
@@ -192,8 +189,12 @@ def tile_self_attention_memory_module_pb_kernel(tc, z, h, m, Wm, bm, out_0, out_
                 "gate_o": squash(acc_o, ACT.Sigmoid, r, OUT_GATE, "gate_o"),
             }
 
+        def memory_of(unit):
+            b, cols = pixels_of(unit["n"])
+            return m_sb[b][:, unit["r"], cols]
+
         def difference(unit):
-            nc.vector.tensor_sub(out=unit["cand"][:], in0=unit["cand"][:], in1=m_sb[unit["n"]][:, unit["r"], :])
+            nc.vector.tensor_sub(out=unit["cand"][:], in0=unit["cand"][:], in1=memory_of(unit))
 
         def gated_step(unit):
             nc.vector.tensor_mul(out=unit["cand"][:], in0=unit["gate_i"][:], in1=unit["cand"][:])
@@ -204,7 +205,7 @@ def tile_self_attention_memory_module_pb_kernel(tc, z, h, m, Wm, bm, out_0, out_
 
         def new_memory(unit):
             new_m = gates.tile([P, N_TILE], F32, name="new_m")
-            nc.vector.tensor_add(out=new_m[:], in0=unit["cand"][:], in1=m_sb[unit["n"]][:, unit["r"], :])
+            nc.vector.tensor_add(out=new_m[:], in0=unit["cand"][:], in1=memory_of(unit))
             store(new_m_tiles, unit, new_m)
             return new_m
 
@@ -212,20 +213,21 @@ def tile_self_attention_memory_module_pb_kernel(tc, z, h, m, Wm, bm, out_0, out_
             nc.vector.tensor_mul(out=unit["gate_o"][:], in0=unit["gate_o"][:], in1=new_m[:])
             store(new_h_tiles, unit, unit["gate_o"])
 
-        copied = None
-        for j in range(W_BANKS):
-            w_grouped = turn_w_bank(j)
-            if copied is not None:
-                quantise_w(*copied)
-            copied = (j, w_grouped)
-        quantise_w(*copied)
-        copied = None
-        for g in range(PASSES):
-            x_grouped = regroup_x(0, g)
-            if copied is not None:
-                quantise_x(*copied)
-            copied = (0, g, x_grouped)
+        for step in range(HEAD_STEPS):
+            first_half = regroup_x(0, step)
+            second_half = regroup_x(1, step)
+            quantise_x(0, step, first_half)
+            quantise_x(1, step, second_half)
+            copied = None
+            for j in range(step * W_BANKS // GATES, (step + 1) * W_BANKS // GATES):
+                w_grouped = turn_w_bank(j)
+                if copied is not None:
+                    quantise_w(*copied)
+                copied = (j, w_grouped)
+            quantise_w(*copied)
 
+        later_pieces = [(n, g) for n in range(HALVES, N_TILES) for g in range(PASSES)]
+        copied = None
         earlier = None
         for n in range(N_TILES):
             for r in range(C_TILES):
@@ -233,8 +235,10 @@ def tile_self_attention_memory_module_pb_kernel(tc, z, h, m, Wm, bm, out_0, out_
                     quantise_x(*copied)
                     copied = None
                 unit = gates_of(n, r)
-                if n + 1 < N_TILES and r < PASSES:
-                    copied = (n + 1, r, regroup_x(n + 1, r))
+                turn, odd = divmod(n * C_TILES + r, 2)
+                if odd == 0 and turn < len(later_pieces):
+                    piece = later_pieces[turn]
+                    copied = (piece[0], piece[1], regroup_x(*piece))
                 difference(unit)
                 if earlier is not None:
                     new_m = new_memory(earlier)

from contextlib import ExitStack

import concourse.mybir as mybir
from concourse.masks import make_identity

F32 = mybir.dt.float32
BF16 = mybir.dt.bfloat16
U32 = mybir.dt.uint32
U8 = mybir.dt.uint8
FP8X4 = mybir.dt.float8_e4m3fn_x4
ACT = mybir.ActivationFunctionType

P = 128
PACK = 4
K_PASS = P * PACK
BATCH = 2
C = 512
C3 = 3 * C
PIXELS = 1024
PASSES = C3 // K_PASS
Z_PASSES = 2
GATES = 3
OUT_GATE, CANDIDATE, IN_GATE = 0, 1, 2
C_TILES = C // P
N_TILE = 512
N_TILES = BATCH * PIXELS // N_TILE
HALVES = PIXELS // N_TILE
PSUM_BANKS = 8
W_CHUNKS = GATES * C_TILES * PASSES
CHUNKS_PER_BANK = 2
W_BANKS = W_CHUNKS // CHUNKS_PER_BANK
HEAD_STEPS = 3
assert HEAD_STEPS == PASSES and HEAD_STEPS == GATES
RUN = 4

FLOPS = 2 * C3 * C3 * BATCH * PIXELS


def tile_self_attention_memory_module_pb_kernel(tc, z, h, m, Wm, bm, out_0, out_1):
    nc = tc.nc

    z_rows = z.rearrange("b c i j -> b c (i j)")
    h_rows = h.rearrange("b c i j -> b c (i j)")
    m_tiles = m.rearrange("b (q r) i j -> b q r (i j)", r=C_TILES)
    new_h_tiles = out_0.rearrange("b (q r) i j -> b q r (i j)", r=C_TILES)
    new_m_tiles = out_1.rearrange("b (q r) i j -> b q r (i j)", r=C_TILES)
    w_tiles = Wm.rearrange("(a q r) k -> a q r k", a=GATES, r=C_TILES)

    def pass_rows(b, g):
        if g < Z_PASSES:
            return z_rows[b, g * K_PASS : (g + 1) * K_PASS, :]
        return h_rows[b]

    def pixels_of(n):
        b, half = divmod(n, HALVES)
        return b, slice(half * N_TILE, (half + 1) * N_TILE)

    with ExitStack() as ctx:
        consts = ctx.enter_context(tc.tile_pool(name="consts", bufs=1))
        resident = ctx.enter_context(tc.tile_pool(name="resident", bufs=1))
        stage = ctx.enter_context(tc.tile_pool(name="stage", bufs=3))
        gates = ctx.enter_context(tc.tile_pool(name="gates", bufs=6))
        psum = ctx.enter_context(tc.psum_pool(name="psum", bufs=PSUM_BANKS))

        w_raw = resident.tile([P, GATES, C_TILES, C3], BF16)
        x_raw = [
            resident.tile([P, PASSES, PACK, PIXELS], BF16, name="x_raw%d" % b) for b in range(BATCH)
        ]
        m_sb = [resident.tile([P, C_TILES, PIXELS], BF16, name="m_sb%d" % b) for b in range(BATCH)]
        w_codes = resident.tile([P, W_CHUNKS * P], U32, align_bytes=64)
        w_scales = resident.tile([P, W_CHUNKS * P], U8, align_bytes=64)
        x_codes = [
            resident.tile([P, PASSES * N_TILE], U32, name="x_codes%d" % n, align_bytes=64)
            for n in range(N_TILES)
        ]
        x_scales = [
            resident.tile([P, PASSES * N_TILE], U8, name="x_scales%d" % n, align_bytes=64)
            for n in range(N_TILES)
        ]

        def load_w(a):
            for first_tile in range(0, C_TILES, 2):
                tiles = slice(first_tile, first_tile + 2)
                nc.sync.dma_start(out=w_raw[:, a, tiles, :], in_=w_tiles[a][:, tiles, :])

        def load_x(b, g):
            nc.sync.dma_start(
                out=x_raw[b][:, g, :, :].rearrange("p (u e) w -> p u (e w)", u=2),
                in_=pass_rows(b, g).rearrange("(u p e) w -> p u (e w)", u=2, e=2),
            )

        def load_m(b):
            nc.sync.dma_start(out=m_sb[b][:], in_=m_tiles[b])

        bias_in = consts.tile([P, GATES, C_TILES], BF16)
        nc.scalar.dma_start(out=bias_in[:], in_=bm.rearrange("(a q r) -> q a r", a=GATES, r=C_TILES))
        for step in range(HEAD_STEPS):
            load_x(0, step)
            load_w(step)
        load_m(0)
        for g in range(PASSES):
            load_x(1, g)
        load_m(1)

        warm = consts.tile([P, 1], F32)
        nc.vector.memset(warm[:], 0.0)
        warm_out = consts.tile([P, 1], F32)
        nc.scalar.activation(out=warm_out[:], in_=warm[:], func=ACT.Sigmoid)

        ident = consts.tile([P, P], F32)
        make_identity(nc, ident[:])

        bias = consts.tile([P, GATES, C_TILES], F32)
        nc.vector.tensor_copy(out=bias[:], in_=bias_in[:])

        def chunk_of(a, r, g):
            return (a * C_TILES + r) * PASSES + g

        def turn_w_bank(j):
            w_turned = psum.tile([P, CHUNKS_PER_BANK, 2, P], F32, tag="bank")
            for s in range(CHUNKS_PER_BANK):
                row_tile, g = divmod(j * CHUNKS_PER_BANK + s, PASSES)
                a, r = divmod(row_tile, C_TILES)
                words = w_raw[:, a, r, :].bitcast(F32)
                for u in range(2):
                    first = g * 2 * P + u * P
                    nc.tensor.transpose(w_turned[:, s, u, :], words[:, first : first + P], ident[:])
            w_grouped = stage.tile([P, CHUNKS_PER_BANK * P * PACK], BF16, align_bytes=64)
            nc.scalar.copy(
                out=w_grouped[:].bitcast(F32).rearrange("p (s o u) -> p s o u", s=CHUNKS_PER_BANK, u=2),
                in_=w_turned[:].rearrange("p s u o -> p s o u"),
            )
            return w_grouped

        def quantise_w(j, w_grouped):
            cols = slice(j * CHUNKS_PER_BANK * P, (j + 1) * CHUNKS_PER_BANK * P)
            nc.vector.quantize_mx(
                out=w_codes[:, cols].bitcast(FP8X4), scales=w_scales[:, cols], in_=w_grouped[:]
            )

        def regroup_x(n, g):
            copy = nc.vector.tensor_copy if n < HALVES else nc.scalar.copy
            b, cols = pixels_of(n)
            x_grouped = stage.tile([P, N_TILE, PACK], BF16, align_bytes=64)
            copy(
                out=x_grouped[:].rearrange("p (c i) t -> p c t i", i=RUN),
                in_=x_raw[b][:, g, :, cols].rearrange("p t (c i) -> p c t i", i=RUN),
            )
            return x_grouped

        def quantise_x(n, g, x_grouped):
            cols = slice(g * N_TILE, (g + 1) * N_TILE)
            nc.vector.quantize_mx(
                out=x_codes[n][:, cols].bitcast(FP8X4),
                scales=x_scales[n][:, cols],
                in_=x_grouped[:].rearrange("p w t -> p (w t)"),
            )

        def multiply(n, r, a):
            acc = psum.tile([P, N_TILE], F32, tag="bank")
            for g in range(PASSES):
                w_cols = slice(chunk_of(a, r, g) * P, (chunk_of(a, r, g) + 1) * P)
                x_cols = slice(g * N_TILE, (g + 1) * N_TILE)
                nc.tensor.matmul_mx(
                    out=acc[:],
                    lhsT=w_codes[:, w_cols].bitcast(FP8X4),
                    lhsT_scale=w_scales[:, w_cols],
                    rhs=x_codes[n][:, x_cols].bitcast(FP8X4),
                    rhs_scale=x_scales[n][:, x_cols],
                    start=(g == 0),
                    stop=(g == PASSES - 1),
                )
            return acc

        def squash(acc, func, r, a, name):
            result = gates.tile([P, N_TILE], F32, name=name)
            nc.scalar.activation(out=result[:], in_=acc[:], func=func, bias=bias[:, a, r : r + 1], scale=1.0)
            return result

        def gates_of(n, r):
            acc_g = multiply(n, r, CANDIDATE)
            acc_i = multiply(n, r, IN_GATE)
            acc_o = multiply(n, r, OUT_GATE)
            return {
                "n": n,
                "r": r,
                "cand": squash(acc_g, ACT.Tanh, r, CANDIDATE, "cand"),
                "gate_i": squash(acc_i, ACT.Sigmoid, r, IN_GATE, "gate_i"),
                "gate_o": squash(acc_o, ACT.Sigmoid, r, OUT_GATE, "gate_o"),
            }

        def memory_of(unit):
            b, cols = pixels_of(unit["n"])
            return m_sb[b][:, unit["r"], cols]

        def difference(unit):
            nc.vector.tensor_sub(out=unit["cand"][:], in0=unit["cand"][:], in1=memory_of(unit))

        def gated_step(unit):
            nc.vector.tensor_mul(out=unit["cand"][:], in0=unit["gate_i"][:], in1=unit["cand"][:])

        def store(tiles, unit, result):
            b, cols = pixels_of(unit["n"])
            nc.sync.dma_start(out=tiles[b][:, unit["r"], cols], in_=result[:])

        def new_memory(unit):
            new_m = gates.tile([P, N_TILE], F32, name="new_m")
            nc.vector.tensor_add(out=new_m[:], in0=unit["cand"][:], in1=memory_of(unit))
            store(new_m_tiles, unit, new_m)
            return new_m

        def new_hidden(unit, new_m):
            nc.vector.tensor_mul(out=unit["gate_o"][:], in0=unit["gate_o"][:], in1=new_m[:])
            store(new_h_tiles, unit, unit["gate_o"])

        for step in range(HEAD_STEPS):
            first_half = regroup_x(0, step)
            second_half = regroup_x(1, step)
            quantise_x(0, step, first_half)
            quantise_x(1, step, second_half)
            copied = None
            for j in range(step * W_BANKS // GATES, (step + 1) * W_BANKS // GATES):
                w_grouped = turn_w_bank(j)
                if copied is not None:
                    quantise_w(*copied)
                copied = (j, w_grouped)
            quantise_w(*copied)

        later_pieces = [(n, g) for n in range(HALVES, N_TILES) for g in range(PASSES)]
        copied = None
        earlier = None
        for n in range(N_TILES):
            for r in range(C_TILES):
                if copied is not None:
                    quantise_x(*copied)
                    copied = None
                unit = gates_of(n, r)
                turn, odd = divmod(n * C_TILES + r, 2)
                if odd == 0 and turn < len(later_pieces):
                    piece = later_pieces[turn]
                    copied = (piece[0], piece[1], regroup_x(*piece))
                difference(unit)
                if earlier is not None:
                    new_m = new_memory(earlier)
                gated_step(unit)
                if earlier is not None:
                    new_hidden(earlier, new_m)
                earlier = unit
        new_hidden(earlier, new_memory(earlier))
